import numpy as np
import ml_dtypes


def mxq(x, axis, fmt="e4m3"):
    dtype, down = {"e4m3": (ml_dtypes.float8_e4m3fn, 7), "e5m2": (ml_dtypes.float8_e5m2, 14)}[fmt]
    v = np.moveaxis(np.asarray(x, np.float32).astype(ml_dtypes.bfloat16).astype(np.float64), axis, -1)
    blocks = v.reshape(v.shape[:-1] + (-1, 32))
    amax = np.abs(blocks).max(-1, keepdims=True)
    byte = np.maximum(np.where(amax > 0, np.frexp(amax)[1] - 1 + 127, 0) - down, 1)
    scale = np.exp2(byte - 127.0)
    codes = (blocks / scale).astype(np.float32).astype(dtype).astype(np.float64)
    return np.moveaxis((codes * scale).reshape(v.shape), -1, axis)


WIDE = False


def mx_kscale(k):
    if not WIDE:
        return np.ones(k)
    levels = np.array([10, -10, 5, -5, 0])
    if k % 512:
        return np.exp2(np.random.permutation(np.resize(levels, k // 32))).repeat(32)
    a = np.empty((k // 512, 16))
    for p in range(k // 512):
        a[p, :8] = np.random.permutation(np.resize(levels, 8))
        for g in range(8):
            far = levels[np.abs(levels - a[p, g]) >= 10]
            a[p, g + 8] = far[np.random.randint(len(far))]
    return np.exp2(a.ravel()).repeat(32)


BF16 = ml_dtypes.bfloat16


def bf(x):
    return np.asarray(x, np.float32).astype(BF16)


def f64(x):
    return np.asarray(x).astype(np.float64)


B, N, F, O, E, K = 4, 512, 512, 64, 16, 3


def normalize_adj(a):
    a = np.maximum(a, 0.0) + np.eye(N)[None, :, :]
    d = np.maximum(a.sum(-1), 1e-6)
    r = d ** -0.5
    return r[:, :, None] * a * r[:, None, :]


def setup_inputs():
    s = mx_kscale(N)
    u = (s / s.min()) ** 2
    x = 0.7 * np.random.standard_normal((B, N, F)) + 0.7 * np.random.standard_normal((B, 1, F))
    x = x * (s / s.max())[None, :, None]
    a0 = 0.5 * (np.random.standard_normal((B, N, N)) - 1.0)
    a = u[None, :, None] * a0
    i = np.arange(N)
    a[:, i, i] = u[None, :] * (np.maximum(a0[:, i, i], 0.0) + 1.0) - 1.0
    return {"A": bf(a), "x": bf(x)}


def reference(A, x):
    a_hat = normalize_adj(f64(A))
    a_left = mxq(a_hat, 2, "e4m3")
    xq = mxq(f64(x), 1, "e4m3")
    t2 = 2.0 * (a_left @ mxq(a_hat, 1, "e4m3")) - np.eye(N)[None, :, :]
    xg1 = a_left @ xq
    xg2 = mxq(t2, 2, "e4m3") @ xq
    return np.stack([xg1, xg2], axis=1)

@@ -1,0 +1,228 @@
+from contextlib import ExitStack
+
+import concourse.mybir as mybir
+from concourse.masks import make_identity
+
+BF16 = mybir.dt.bfloat16
+F32 = mybir.dt.float32
+U32 = mybir.dt.uint32
+U8 = mybir.dt.uint8
+FP8X4 = mybir.dt.float8_e4m3fn_x4
+ACT = mybir.ActivationFunctionType
+ALU = mybir.AluOpType
+
+P = 128
+PACK = 4
+GRAPHS = 4
+NODES = P * PACK
+FEATS = 512
+DIAG_STEP = NODES + P
+
+FLOPS = 3 * GRAPHS * 2 * NODES * NODES * FEATS
+
+
+def tile_dygcn_pa_kernel(tc, A, x, out):
+    nc = tc.nc
+    with ExitStack() as ctx:
+        consts = ctx.enter_context(tc.tile_pool(name="consts", bufs=1))
+        loads = ctx.enter_context(tc.tile_pool(name="loads", bufs=GRAPHS))
+        ahead = ctx.enter_context(tc.tile_pool(name="ahead", bufs=3))
+        work = ctx.enter_context(tc.tile_pool(name="work", bufs=2))
+        results = ctx.enter_context(tc.tile_pool(name="results", bufs=8))
+        psum_row = ctx.enter_context(tc.psum_pool(name="psum_row", bufs=1))
+        psum_flip = ctx.enter_context(tc.psum_pool(name="psum_flip", bufs=2))
+        psum_acc = ctx.enter_context(tc.psum_pool(name="psum_acc", bufs=5))
+
+        def block(i):
+            return slice(i * P, (i + 1) * P)
+
+        a_raw = []
+        x_raw = []
+        for b in range(GRAPHS):
+            a_tile = loads.tile([P, PACK, NODES], BF16, name="a_raw")
+            for t in range(PACK):
+                nc.sync.dma_start(out=a_tile[:, t, :], in_=A[b].rearrange("(p t) m -> t p m", t=PACK)[t])
+            a_raw.append(a_tile)
+            x_tile = loads.tile([P, PACK, FEATS], BF16, name="x_raw")
+            nc.sync.dma_start(out=x_tile[:], in_=x[b].rearrange("(p t) f -> p t f", t=PACK))
+            x_raw.append(x_tile)
+
+        warm = consts.tile([P, 1], F32)
+        nc.vector.memset(warm[:], 1.0)
+        nc.scalar.activation(out=warm[:], in_=warm[:], func=ACT.Sqrt)
+        ident_f32 = consts.tile([P, P], F32)
+        make_identity(nc, ident_f32[:])
+        ident_bf16 = consts.tile([P, P], BF16)
+        make_identity(nc, ident_bf16[:])
+        eye_grouped = consts.tile([P, PACK, P, PACK], BF16)
+        nc.vector.memset(eye_grouped[:], 0.0)
+        for i in range(PACK):
+            nc.vector.tensor_copy(out=eye_grouped[:, i, :, i], in_=ident_bf16[:])
+
+        def regroup(grouped, rows):
+            nc.vector.tensor_copy(
+                out=grouped[:].rearrange("p (c i) t -> p c t i", i=4),
+                in_=rows[:].rearrange("p t (c i) -> p c t i", i=4),
+            )
+
+        def mx_tiles(name):
+            codes = work.tile([P, NODES], U32, name=name + "_codes", align_bytes=64)
+            scales = work.tile([P, NODES], U8, name=name + "_scales", align_bytes=64)
+            return codes, scales
+
+        def quantise(operand, grouped, cols):
+            nc.vector.quantize_mx(
+                out=operand[0][:, cols].bitcast(FP8X4),
+                scales=operand[1][:, cols],
+                in_=grouped[:, cols, :].rearrange("p w t -> p (w t)"),
+            )
+
+        def multiply(acc, stationary, s_cols, moving, m_cols):
+            nc.tensor.matmul_mx(
+                out=acc,
+                lhsT=stationary[0][:, s_cols].bitcast(FP8X4),
+                lhsT_scale=stationary[1][:, s_cols],
+                rhs=moving[0][:, m_cols].bitcast(FP8X4),
+                rhs_scale=moving[1][:, m_cols],
+                start=True,
+                stop=True,
+            )
+
+        everything = slice(0, NODES)
+        pos = {}
+        row_sum = {}
+        root = {}
+        r = {}
+        r_row = {}
+        left = {}
+        right = {}
+        x_mx = {}
+        x_grouped = {}
+        squares = {}
+
+        def positive_part(b):
+            pos[b] = ahead.tile([P, PACK * DIAG_STEP], F32, name="pos")
+            row_sum[b] = ahead.tile([P, PACK], F32, name="row_sum")
+            for t in range(PACK):
+                nc.scalar.activation(
+                    out=pos[b][:, t * NODES : (t + 1) * NODES].rearrange("p (u w) -> p u w", u=PACK),
+                    in_=a_raw[b][:, t, :].rearrange("p (w u) -> p u w", u=PACK),
+                    func=ACT.Relu,
+                    accum_out=row_sum[b][:, t : t + 1],
+                )
+            diagonal = pos[b][:].rearrange("p (t c) -> p t c", c=DIAG_STEP)[:, :, 0:P]
+            nc.gpsimd.tensor_tensor(
+                out=diagonal,
+                in0=diagonal,
+                in1=ident_f32[:].unsqueeze(1).to_broadcast([P, PACK, P]),
+                op=ALU.add,
+            )
+
+        def degree_root(b):
+            degree = work.tile([P, PACK], F32)
+            nc.vector.tensor_scalar(
+                out=degree[:], in0=row_sum[b][:], scalar1=1.0, scalar2=1e-6, op0=ALU.add, op1=ALU.max
+            )
+            root[b] = work.tile([P, PACK], F32, name="root")
+            nc.scalar.activation(out=root[b][:], in_=degree[:], func=ACT.Sqrt)
+
+        def scale_factors(b):
+            r[b] = work.tile([P, PACK], F32, name="r")
+            nc.vector.reciprocal(out=r[b][:], in_=root[b][:])
+            r_row[b] = psum_row.tile([P, NODES], F32, name="r_row")
+            for t in range(PACK):
+                nc.tensor.transpose(
+                    r_row[b][:, block(t)], r[b][:, t : t + 1].to_broadcast([P, P]), ident_f32[:]
+                )
+
+        def normalise(b):
+            a_hat = work.tile([P, PACK, NODES], BF16)
+            left_grouped = work.tile([P, NODES, PACK], BF16, align_bytes=64)
+            for t in range(PACK):
+                nc.vector.scalar_tensor_tensor(
+                    out=a_hat[:, t, :],
+                    in0=pos[b][:, t * NODES : (t + 1) * NODES],
+                    scalar=r[b][:, t : t + 1],
+                    in1=r_row[b][:],
+                    op0=ALU.mult,
+                    op1=ALU.mult,
+                )
+                flipped = psum_flip.tile([P, PACK, P], BF16)
+                for u in range(PACK):
+                    nc.tensor.transpose(flipped[:, u, :], a_hat[:, t, block(u)], ident_bf16[:])
+                nc.scalar.copy(
+                    out=left_grouped[:, block(t), :], in_=flipped[:].rearrange("p u w -> p w u")
+                )
+            return a_hat, left_grouped
+
+        def product_with_x(b, which, operand, c):
+            acc = psum_acc.tile([P, FEATS], F32, tag="acc", name="product")
+            multiply(acc[:], operand, block(c), x_mx[b], everything)
+            res = results.tile([P, FEATS], F32)
+            nc.scalar.copy(out=res[:], in_=acc[:])
+            nc.sync.dma_start(out=out[b, which].rearrange("(w i) f -> i w f", i=PACK)[c], in_=res[:])
+
+        def regroup_x(b):
+            x_grouped[b] = work.tile([P, FEATS, PACK], BF16, name="x_grouped", align_bytes=64)
+            regroup(x_grouped[b], x_raw[b])
+
+        def quantise_x(b):
+            x_mx[b] = mx_tiles("x")
+            quantise(x_mx[b], x_grouped[b], everything)
+
+        def make_operands(b, a_hat, left_grouped):
+            right_grouped = work.tile([P, NODES, PACK], BF16, align_bytes=64)
+            regroup(right_grouped, a_hat)
+            left[b] = mx_tiles("left")
+            quantise(left[b], left_grouped, everything)
+            for c in range(PACK):
+                product_with_x(b, 0, left[b], c)
+            if b + 1 < GRAPHS:
+                regroup_x(b + 1)
+            right[b] = mx_tiles("right")
+            quantise(right[b], right_grouped, everything)
+            if b + 1 < GRAPHS:
+                quantise_x(b + 1)
+            squares[b] = []
+            for i in range(PACK):
+                acc = psum_acc.tile([P, PACK, P], F32, tag="acc", name="square")
+                for t in range(PACK):
+                    multiply(acc[:, t, :], right[b], block(t), left[b], block(i))
+                squares[b].append(acc)
+
+        def products(b):
+            t2_grouped = work.tile([P, NODES, PACK], BF16, align_bytes=64)
+            t2_mx = mx_tiles("t2")
+            for i in range(PACK + 1):
+                if i < PACK:
+                    nc.vector.scalar_tensor_tensor(
+                        out=t2_grouped[:, block(i), :],
+                        in0=squares[b][i][:].rearrange("p t w -> p w t"),
+                        scalar=2.0,
+                        in1=eye_grouped[:, i, :, :],
+                        op0=ALU.mult,
+                        op1=ALU.subtract,
+                    )
+                if i >= 1:
+                    quantise(t2_mx, t2_grouped, block(i - 1))
+                    product_with_x(b, 1, t2_mx, i - 1)
+
+        positive_part(0)
+        regroup_x(0)
+        degree_root(0)
+        scale_factors(0)
+        quantise_x(0)
+        positive_part(1)
+        for b in range(GRAPHS + 1):
+            if b < GRAPHS:
+                a_hat, left_grouped = normalise(b)
+            if b + 1 < GRAPHS:
+                degree_root(b + 1)
+            if b >= 1:
+                products(b - 1)
+            if b + 1 < GRAPHS:
+                scale_factors(b + 1)
+            if b < GRAPHS:
+                make_operands(b, a_hat, left_grouped)
+            if b + 2 < GRAPHS:
+                positive_part(b + 2)

@@ -65,6 +65,12 @@ def tile_dygcn_pa_kernel(tc, A, x, out):
                 in_=rows[:].rearrange("p t (c i) -> p c t i", i=4),
             )
 
+        def regroup_permuted(grouped, rows):
+            nc.vector.tensor_copy(
+                out=grouped[:].rearrange("p (u w) t -> p u w t", u=PACK),
+                in_=rows[:].rearrange("p t (w u) -> p u w t", u=PACK),
+            )
+
         def mx_tiles(name):
             codes = work.tile([P, NODES], U32, name=name + "_codes", align_bytes=64)
             scales = work.tile([P, NODES], U8, name=name + "_scales", align_bytes=64)
@@ -140,18 +146,20 @@ def tile_dygcn_pa_kernel(tc, A, x, out):
             left_grouped = work.tile([P, NODES, PACK], BF16, align_bytes=64)
             for t in range(PACK):
                 nc.vector.scalar_tensor_tensor(
-                    out=a_hat[:, t, :],
-                    in0=pos[b][:, t * NODES : (t + 1) * NODES],
+                    out=a_hat[:, t, :].rearrange("p (w u) -> p w u", u=PACK),
+                    in0=pos[b][:, t * NODES : (t + 1) * NODES].rearrange("p (u w) -> p w u", u=PACK),
                     scalar=r[b][:, t : t + 1],
-                    in1=r_row[b][:],
+                    in1=r_row[b][:].rearrange("p (u w) -> p w u", u=PACK),
                     op0=ALU.mult,
                     op1=ALU.mult,
                 )
-                flipped = psum_flip.tile([P, PACK, P], BF16)
-                for u in range(PACK):
-                    nc.tensor.transpose(flipped[:, u, :], a_hat[:, t, block(u)], ident_bf16[:])
+                words = a_hat[:, t, :].bitcast(F32)
+                flipped = psum_flip.tile([P, 2, P], F32)
+                for h in range(2):
+                    nc.tensor.transpose(flipped[:, h, :], words[:, h : NODES // 2 : 2], ident_f32[:])
                 nc.scalar.copy(
-                    out=left_grouped[:, block(t), :], in_=flipped[:].rearrange("p u w -> p w u")
+                    out=left_grouped[:, block(t), :].rearrange("p w u -> p (w u)").bitcast(F32).rearrange("p (w h) -> p w h", h=2),
+                    in_=flipped[:].rearrange("p h w -> p w h"),
                 )
             return a_hat, left_grouped
 
@@ -172,7 +180,7 @@ def tile_dygcn_pa_kernel(tc, A, x, out):
 
         def make_operands(b, a_hat, left_grouped):
             right_grouped = work.tile([P, NODES, PACK], BF16, align_bytes=64)
-            regroup(right_grouped, a_hat)
+            regroup_permuted(right_grouped, a_hat)
             left[b] = mx_tiles("left")
             quantise(left[b], left_grouped, everything)
             for c in range(PACK):

@@ -26,12 +26,11 @@ def tile_dygcn_pa_kernel(tc, A, x, out):
     with ExitStack() as ctx:
         consts = ctx.enter_context(tc.tile_pool(name="consts", bufs=1))
         loads = ctx.enter_context(tc.tile_pool(name="loads", bufs=GRAPHS))
-        ahead = ctx.enter_context(tc.tile_pool(name="ahead", bufs=3))
         work = ctx.enter_context(tc.tile_pool(name="work", bufs=2))
-        results = ctx.enter_context(tc.tile_pool(name="results", bufs=8))
-        psum_row = ctx.enter_context(tc.psum_pool(name="psum_row", bufs=1))
-        psum_flip = ctx.enter_context(tc.psum_pool(name="psum_flip", bufs=2))
-        psum_acc = ctx.enter_context(tc.psum_pool(name="psum_acc", bufs=5))
+        operands = ctx.enter_context(tc.tile_pool(name="operands", bufs=3))
+        results = ctx.enter_context(tc.tile_pool(name="results", bufs=12))
+        psum = ctx.enter_context(tc.psum_pool(name="psum", bufs=8))
+        ctx.enter_context(tc.manual_schedule())
 
         def block(i):
             return slice(i * P, (i + 1) * P)
@@ -40,8 +39,12 @@ def tile_dygcn_pa_kernel(tc, A, x, out):
         x_raw = []
         for b in range(GRAPHS):
             a_tile = loads.tile([P, PACK, NODES], BF16, name="a_raw")
-            for t in range(PACK):
-                nc.sync.dma_start(out=a_tile[:, t, :], in_=A[b].rearrange("(p t) m -> t p m", t=PACK)[t])
+            rows = A[b].rearrange("(p t) m -> p t m", t=PACK)
+            if b == 0:
+                for t in range(PACK):
+                    nc.sync.dma_start(out=a_tile[:, t, :], in_=rows[:, t, :])
+            else:
+                nc.sync.dma_start(out=a_tile[:], in_=rows)
             a_raw.append(a_tile)
             x_tile = loads.tile([P, PACK, FEATS], BF16, name="x_raw")
             nc.sync.dma_start(out=x_tile[:], in_=x[b].rearrange("(p t) f -> p t f", t=PACK))
@@ -49,31 +52,19 @@ def tile_dygcn_pa_kernel(tc, A, x, out):
 
         warm = consts.tile([P, 1], F32)
         nc.vector.memset(warm[:], 1.0)
-        nc.scalar.activation(out=warm[:], in_=warm[:], func=ACT.Sqrt)
+        nc.scalar.activation(out=warm[:], in_=warm[:], func=ACT.Abs_reciprocal_sqrt)
         ident_f32 = consts.tile([P, P], F32)
         make_identity(nc, ident_f32[:])
-        ident_bf16 = consts.tile([P, P], BF16)
-        make_identity(nc, ident_bf16[:])
         eye_grouped = consts.tile([P, PACK, P, PACK], BF16)
-        nc.vector.memset(eye_grouped[:], 0.0)
+        nc.vector.memset(eye_grouped[:].rearrange("p i w t -> p (i w t)").bitcast(F32), 0.0)
+        ident_bf16 = consts.tile([P, P], BF16)
+        nc.vector.tensor_copy(out=ident_bf16[:], in_=ident_f32[:])
         for i in range(PACK):
-            nc.vector.tensor_copy(out=eye_grouped[:, i, :, i], in_=ident_bf16[:])
-
-        def regroup(grouped, rows):
-            nc.vector.tensor_copy(
-                out=grouped[:].rearrange("p (c i) t -> p c t i", i=4),
-                in_=rows[:].rearrange("p t (c i) -> p c t i", i=4),
-            )
-
-        def regroup_permuted(grouped, rows):
-            nc.vector.tensor_copy(
-                out=grouped[:].rearrange("p (u w) t -> p u w t", u=PACK),
-                in_=rows[:].rearrange("p t (w u) -> p u w t", u=PACK),
-            )
+            nc.vector.tensor_copy(out=eye_grouped[:, i, :, i], in_=ident_f32[:])
 
         def mx_tiles(name):
-            codes = work.tile([P, NODES], U32, name=name + "_codes", align_bytes=64)
-            scales = work.tile([P, NODES], U8, name=name + "_scales", align_bytes=64)
+            codes = operands.tile([P, NODES], U32, name=name + "_codes", align_bytes=64)
+            scales = operands.tile([P, NODES], U8, name=name + "_scales", align_bytes=64)
             return codes, scales
 
         def quantise(operand, grouped, cols):
@@ -97,140 +88,167 @@ def tile_dygcn_pa_kernel(tc, A, x, out):
         everything = slice(0, NODES)
         pos = {}
         row_sum = {}
-        root = {}
         r = {}
         r_row = {}
+        a_hat = {}
+        left_grouped = {}
+        flipped = {}
         left = {}
-        right = {}
         x_mx = {}
         x_grouped = {}
         squares = {}
 
-        def positive_part(b):
-            pos[b] = ahead.tile([P, PACK * DIAG_STEP], F32, name="pos")
-            row_sum[b] = ahead.tile([P, PACK], F32, name="row_sum")
-            for t in range(PACK):
-                nc.scalar.activation(
-                    out=pos[b][:, t * NODES : (t + 1) * NODES].rearrange("p (u w) -> p u w", u=PACK),
-                    in_=a_raw[b][:, t, :].rearrange("p (w u) -> p u w", u=PACK),
-                    func=ACT.Relu,
-                    accum_out=row_sum[b][:, t : t + 1],
+        def start_positive_part(b):
+            pos[b] = work.tile([P, PACK * DIAG_STEP], F32, name="pos")
+            row_sum[b] = work.tile([P, PACK], F32, name="row_sum")
+
+        def positive_part(b, t, on_vector=False):
+            relu_out = pos[b][:, t * NODES : (t + 1) * NODES].rearrange("p (u w) -> p u w", u=PACK)
+            relu_in = a_raw[b][:, t, :].rearrange("p (w u) -> p u w", u=PACK)
+            total = row_sum[b][:, t : t + 1]
+            if on_vector:
+                nc.vector.tensor_scalar(
+                    out=relu_out, in0=relu_in, scalar1=0.0, scalar2=None, op0=ALU.max, op1=ALU.add, accum_out=total
                 )
-            diagonal = pos[b][:].rearrange("p (t c) -> p t c", c=DIAG_STEP)[:, :, 0:P]
-            nc.gpsimd.tensor_tensor(
-                out=diagonal,
-                in0=diagonal,
-                in1=ident_f32[:].unsqueeze(1).to_broadcast([P, PACK, P]),
-                op=ALU.add,
-            )
+            else:
+                nc.scalar.activation(out=relu_out, in_=relu_in, func=ACT.Relu, accum_out=total)
+            diag = pos[b][:, t * DIAG_STEP : t * DIAG_STEP + P]
+            nc.gpsimd.tensor_tensor(out=diag, in0=diag, in1=ident_f32[:], op=ALU.add)
 
-        def degree_root(b):
-            degree = work.tile([P, PACK], F32)
-            nc.vector.tensor_scalar(
-                out=degree[:], in0=row_sum[b][:], scalar1=1.0, scalar2=1e-6, op0=ALU.add, op1=ALU.max
-            )
-            root[b] = work.tile([P, PACK], F32, name="root")
-            nc.scalar.activation(out=root[b][:], in_=degree[:], func=ACT.Sqrt)
-
-        def scale_factors(b):
+        def factors(b):
             r[b] = work.tile([P, PACK], F32, name="r")
-            nc.vector.reciprocal(out=r[b][:], in_=root[b][:])
-            r_row[b] = psum_row.tile([P, NODES], F32, name="r_row")
-            for t in range(PACK):
-                nc.tensor.transpose(
-                    r_row[b][:, block(t)], r[b][:, t : t + 1].to_broadcast([P, P]), ident_f32[:]
-                )
+            nc.scalar.activation(out=r[b][:], in_=row_sum[b][:], func=ACT.Abs_reciprocal_sqrt, bias=1.0)
 
-        def normalise(b):
-            a_hat = work.tile([P, PACK, NODES], BF16)
-            left_grouped = work.tile([P, NODES, PACK], BF16, align_bytes=64)
+        def factors_row(b):
+            r_row[b] = psum.tile([P, NODES], F32, tag="bank", name="r_row")
             for t in range(PACK):
-                nc.vector.scalar_tensor_tensor(
-                    out=a_hat[:, t, :].rearrange("p (w u) -> p w u", u=PACK),
-                    in0=pos[b][:, t * NODES : (t + 1) * NODES].rearrange("p (u w) -> p w u", u=PACK),
-                    scalar=r[b][:, t : t + 1],
-                    in1=r_row[b][:].rearrange("p (u w) -> p w u", u=PACK),
-                    op0=ALU.mult,
-                    op1=ALU.mult,
-                )
-                words = a_hat[:, t, :].bitcast(F32)
-                flipped = psum_flip.tile([P, 2, P], F32)
-                for h in range(2):
-                    nc.tensor.transpose(flipped[:, h, :], words[:, h : NODES // 2 : 2], ident_f32[:])
+                nc.tensor.transpose(r_row[b][:, block(t)], r[b][:, t : t + 1].to_broadcast([P, P]), ident_f32[:])
+
+        def start_normalise(b):
+            a_hat[b] = work.tile([P, PACK, NODES], BF16, name="a_hat")
+            left_grouped[b] = work.tile([P, NODES, PACK], BF16, name="left_grouped", align_bytes=64)
+
+        def normalise(b, t):
+            nc.vector.scalar_tensor_tensor(
+                out=a_hat[b][:, t, :].rearrange("p (w u) -> p w u", u=PACK),
+                in0=pos[b][:, t * NODES : (t + 1) * NODES].rearrange("p (u w) -> p w u", u=PACK),
+                scalar=r[b][:, t : t + 1],
+                in1=r_row[b][:].rearrange("p (u w) -> p w u", u=PACK),
+                op0=ALU.mult,
+                op1=ALU.mult,
+            )
+            words = a_hat[b][:, t, :].bitcast(F32)
+            if t % 2 == 0:
+                flipped[b] = psum.tile([P, 2, 2, P], F32, tag="bank", name="flipped")
+            for h in range(2):
+                nc.tensor.transpose(flipped[b][:, t % 2, h, :], words[:, h : NODES // 2 : 2], ident_f32[:])
+            if t % 2 == 1:
                 nc.scalar.copy(
-                    out=left_grouped[:, block(t), :].rearrange("p w u -> p (w u)").bitcast(F32).rearrange("p (w h) -> p w h", h=2),
-                    in_=flipped[:].rearrange("p h w -> p w h"),
+                    out=left_grouped[b][:, (t - 1) * P : (t + 1) * P, :].rearrange("p w u -> p (w u)").bitcast(F32).rearrange("p (s w h) -> p s w h", s=2, h=2),
+                    in_=flipped[b][:].rearrange("p s h w -> p s w h"),
                 )
-            return a_hat, left_grouped
 
-        def product_with_x(b, which, operand, c):
-            acc = psum_acc.tile([P, FEATS], F32, tag="acc", name="product")
+        def product_with_x(b, which, operand, c, on_vector=False):
+            acc = psum.tile([P, FEATS], F32, tag="bank", name="product")
             multiply(acc[:], operand, block(c), x_mx[b], everything)
             res = results.tile([P, FEATS], F32)
-            nc.scalar.copy(out=res[:], in_=acc[:])
+            if on_vector:
+                nc.vector.tensor_copy(out=res[:], in_=acc[:])
+            else:
+                nc.scalar.copy(out=res[:], in_=acc[:])
             nc.sync.dma_start(out=out[b, which].rearrange("(w i) f -> i w f", i=PACK)[c], in_=res[:])
 
         def regroup_x(b):
             x_grouped[b] = work.tile([P, FEATS, PACK], BF16, name="x_grouped", align_bytes=64)
-            regroup(x_grouped[b], x_raw[b])
+            if b == 0:
+                nc.vector.tensor_copy(
+                    out=x_grouped[b][:].rearrange("p (c i) t -> p c t i", i=4),
+                    in_=x_raw[b][:].rearrange("p t (c i) -> p c t i", i=4),
+                )
+                return
+            for f0 in range(0, FEATS, 2 * P):
+                gathered = psum.tile([P, 2, P, PACK], BF16, tag="bank", name="gathered")
+                for k in range(2):
+                    nc.tensor.matmul(
+                        out=gathered[:, k, :, :],
+                        lhsT=ident_bf16[:],
+                        rhs=x_raw[b][:, :, f0 + k * P : f0 + (k + 1) * P].rearrange("p t f -> p f t"),
+                        start=True,
+                        stop=True,
+                    )
+                nc.scalar.copy(
+                    out=x_grouped[b][:, f0 : f0 + 2 * P, :].rearrange("p f t -> p (f t)").bitcast(F32),
+                    in_=gathered[:].rearrange("p k f t -> p (k f t)").bitcast(F32),
+                )
 
         def quantise_x(b):
             x_mx[b] = mx_tiles("x")
             quantise(x_mx[b], x_grouped[b], everything)
 
-        def make_operands(b, a_hat, left_grouped):
-            right_grouped = work.tile([P, NODES, PACK], BF16, align_bytes=64)
-            regroup_permuted(right_grouped, a_hat)
-            left[b] = mx_tiles("left")
-            quantise(left[b], left_grouped, everything)
-            for c in range(PACK):
-                product_with_x(b, 0, left[b], c)
-            if b + 1 < GRAPHS:
-                regroup_x(b + 1)
-            right[b] = mx_tiles("right")
-            quantise(right[b], right_grouped, everything)
-            if b + 1 < GRAPHS:
-                quantise_x(b + 1)
+        def square(b, right):
             squares[b] = []
             for i in range(PACK):
-                acc = psum_acc.tile([P, PACK, P], F32, tag="acc", name="square")
+                acc = psum.tile([P, PACK, P], F32, tag="bank", name="square")
                 for t in range(PACK):
-                    multiply(acc[:, t, :], right[b], block(t), left[b], block(i))
+                    multiply(acc[:, t, :], right, block(t), left[b], block(i))
                 squares[b].append(acc)
 
-        def products(b):
-            t2_grouped = work.tile([P, NODES, PACK], BF16, align_bytes=64)
-            t2_mx = mx_tiles("t2")
-            for i in range(PACK + 1):
-                if i < PACK:
-                    nc.vector.scalar_tensor_tensor(
-                        out=t2_grouped[:, block(i), :],
-                        in0=squares[b][i][:].rearrange("p t w -> p w t"),
-                        scalar=2.0,
-                        in1=eye_grouped[:, i, :, :],
-                        op0=ALU.mult,
-                        op1=ALU.subtract,
-                    )
-                if i >= 1:
-                    quantise(t2_mx, t2_grouped, block(i - 1))
-                    product_with_x(b, 1, t2_mx, i - 1)
-
-        positive_part(0)
+        start_positive_part(0)
+        for t in range(PACK):
+            positive_part(0, t, on_vector=t % 2 == 1)
+        factors(0)
+        factors_row(0)
         regroup_x(0)
-        degree_root(0)
-        scale_factors(0)
-        quantise_x(0)
-        positive_part(1)
         for b in range(GRAPHS + 1):
+            ahead = b + 1 < GRAPHS
+            if ahead:
+                start_positive_part(b + 1)
+            if b == 0:
+                for t in range(PACK):
+                    positive_part(1, t)
             if b < GRAPHS:
-                a_hat, left_grouped = normalise(b)
-            if b + 1 < GRAPHS:
-                degree_root(b + 1)
+                start_normalise(b)
+                for t in range(PACK):
+                    if ahead and b > 0:
+                        positive_part(b + 1, t)
+                    normalise(b, t)
+            if b == 0:
+                quantise_x(0)
+            if ahead:
+                factors(b + 1)
+                regroup_x(b + 1)
+                factors_row(b + 1)
             if b >= 1:
-                products(b - 1)
-            if b + 1 < GRAPHS:
-                scale_factors(b + 1)
+                t2_grouped = work.tile([P, NODES, PACK], BF16, align_bytes=64)
+                t2_mx = mx_tiles("t2")
+                for i in range(PACK + 1):
+                    if i < PACK:
+                        nc.vector.scalar_tensor_tensor(
+                            out=t2_grouped[:, block(i), :],
+                            in0=squares[b - 1][i][:].rearrange("p t w -> p w t"),
+                            scalar=2.0,
+                            in1=eye_grouped[:, i, :, :],
+                            op0=ALU.mult,
+                            op1=ALU.subtract,
+                        )
+                    if i >= 1:
+                        quantise(t2_mx, t2_grouped, block(i - 1))
+                        product_with_x(b - 1, 1, t2_mx, i - 1, on_vector=b == GRAPHS and i == PACK)
             if b < GRAPHS:
-                make_operands(b, a_hat, left_grouped)
-            if b + 2 < GRAPHS:
-                positive_part(b + 2)
+                right_grouped = work.tile([P, NODES, PACK], BF16, align_bytes=64)
+                nc.vector.tensor_copy(
+                    out=right_grouped[:].rearrange("p (u w) t -> p u w t", u=PACK),
+                    in_=a_hat[b][:].rearrange("p t (w u) -> p u w t", u=PACK),
+                )
+                left[b] = mx_tiles("left")
+                quantise(left[b], left_grouped[b], everything)
+                right = mx_tiles("right")
+                quantise(right, right_grouped, everything)
+                for c in range(PACK):
+                    if c == 2 and not ahead:
+                        square(b, right)
+                    product_with_x(b, 0, left[b], c)
+                if ahead:
+                    square(b, right)
+                if ahead:
+                    quantise_x(b + 1)

@@ -16,7 +16,6 @@ PACK = 4
 GRAPHS = 4
 NODES = P * PACK
 FEATS = 512
-DIAG_STEP = NODES + P
 
 FLOPS = 3 * GRAPHS * 2 * NODES * NODES * FEATS
 
@@ -55,12 +54,18 @@ def tile_dygcn_pa_kernel(tc, A, x, out):
         nc.scalar.activation(out=warm[:], in_=warm[:], func=ACT.Abs_reciprocal_sqrt)
         ident_f32 = consts.tile([P, P], F32)
         make_identity(nc, ident_f32[:])
+        eye_pairs = consts.tile([P, 2, 2 * P], F32)
+        nc.vector.memset(eye_pairs[:], 0.0)
         eye_grouped = consts.tile([P, PACK, P, PACK], BF16)
         nc.vector.memset(eye_grouped[:].rearrange("p i w t -> p (i w t)").bitcast(F32), 0.0)
+        for e in range(2):
+            nc.vector.tensor_copy(out=eye_pairs[:, e, e : 2 * P : 2], in_=ident_f32[:])
         ident_bf16 = consts.tile([P, P], BF16)
-        nc.vector.tensor_copy(out=ident_bf16[:], in_=ident_f32[:])
-        for i in range(PACK):
-            nc.vector.tensor_copy(out=eye_grouped[:, i, :, i], in_=ident_f32[:])
+
+        def finish_constants():
+            nc.vector.tensor_copy(out=ident_bf16[:], in_=ident_f32[:])
+            for i in range(PACK):
+                nc.vector.tensor_copy(out=eye_grouped[:, i, :, i], in_=ident_f32[:])
 
         def mx_tiles(name):
             codes = operands.tile([P, NODES], U32, name=name + "_codes", align_bytes=64)
@@ -99,12 +104,12 @@ def tile_dygcn_pa_kernel(tc, A, x, out):
         squares = {}
 
         def start_positive_part(b):
-            pos[b] = work.tile([P, PACK * DIAG_STEP], F32, name="pos")
+            pos[b] = work.tile([P, PACK, NODES], F32, name="pos")
             row_sum[b] = work.tile([P, PACK], F32, name="row_sum")
 
         def positive_part(b, t, on_vector=False):
-            relu_out = pos[b][:, t * NODES : (t + 1) * NODES].rearrange("p (u w) -> p u w", u=PACK)
-            relu_in = a_raw[b][:, t, :].rearrange("p (w u) -> p u w", u=PACK)
+            relu_out = pos[b][:, t, :].rearrange("p (h w e) -> p h w e", h=2, e=2)
+            relu_in = a_raw[b][:, t, :].rearrange("p (w h e) -> p h w e", h=2, e=2)
             total = row_sum[b][:, t : t + 1]
             if on_vector:
                 nc.vector.tensor_scalar(
@@ -112,17 +117,17 @@ def tile_dygcn_pa_kernel(tc, A, x, out):
                 )
             else:
                 nc.scalar.activation(out=relu_out, in_=relu_in, func=ACT.Relu, accum_out=total)
-            diag = pos[b][:, t * DIAG_STEP : t * DIAG_STEP + P]
-            nc.gpsimd.tensor_tensor(out=diag, in0=diag, in1=ident_f32[:], op=ALU.add)
+            half = pos[b][:, t, (t // 2) * 2 * P : (t // 2 + 1) * 2 * P]
+            nc.gpsimd.tensor_tensor(out=half, in0=half, in1=eye_pairs[:, t % 2, :], op=ALU.add)
 
         def factors(b):
             r[b] = work.tile([P, PACK], F32, name="r")
             nc.scalar.activation(out=r[b][:], in_=row_sum[b][:], func=ACT.Abs_reciprocal_sqrt, bias=1.0)
 
         def factors_row(b):
-            r_row[b] = psum.tile([P, NODES], F32, tag="bank", name="r_row")
+            r_row[b] = psum.tile([P, 2, P, 2], F32, tag="bank", name="r_row")
             for t in range(PACK):
-                nc.tensor.transpose(r_row[b][:, block(t)], r[b][:, t : t + 1].to_broadcast([P, P]), ident_f32[:])
+                nc.tensor.transpose(r_row[b][:, t // 2, :, t % 2], r[b][:, t : t + 1].to_broadcast([P, P]), ident_f32[:])
 
         def start_normalise(b):
             a_hat[b] = work.tile([P, PACK, NODES], BF16, name="a_hat")
@@ -130,10 +135,10 @@ def tile_dygcn_pa_kernel(tc, A, x, out):
 
         def normalise(b, t):
             nc.vector.scalar_tensor_tensor(
-                out=a_hat[b][:, t, :].rearrange("p (w u) -> p w u", u=PACK),
-                in0=pos[b][:, t * NODES : (t + 1) * NODES].rearrange("p (u w) -> p w u", u=PACK),
+                out=a_hat[b][:, t, :],
+                in0=pos[b][:, t, :],
                 scalar=r[b][:, t : t + 1],
-                in1=r_row[b][:].rearrange("p (u w) -> p w u", u=PACK),
+                in1=r_row[b][:].rearrange("p h w e -> p (h w e)"),
                 op0=ALU.mult,
                 op1=ALU.mult,
             )
@@ -141,7 +146,7 @@ def tile_dygcn_pa_kernel(tc, A, x, out):
             if t % 2 == 0:
                 flipped[b] = psum.tile([P, 2, 2, P], F32, tag="bank", name="flipped")
             for h in range(2):
-                nc.tensor.transpose(flipped[b][:, t % 2, h, :], words[:, h : NODES // 2 : 2], ident_f32[:])
+                nc.tensor.transpose(flipped[b][:, t % 2, h, :], words[:, block(h)], ident_f32[:])
             if t % 2 == 1:
                 nc.scalar.copy(
                     out=left_grouped[b][:, (t - 1) * P : (t + 1) * P, :].rearrange("p w u -> p (w u)").bitcast(F32).rearrange("p (s w h) -> p s w h", s=2, h=2),
@@ -198,6 +203,7 @@ def tile_dygcn_pa_kernel(tc, A, x, out):
             positive_part(0, t, on_vector=t % 2 == 1)
         factors(0)
         factors_row(0)
+        finish_constants()
         regroup_x(0)
         for b in range(GRAPHS + 1):
             ahead = b + 1 < GRAPHS
@@ -236,10 +242,12 @@ def tile_dygcn_pa_kernel(tc, A, x, out):
                         product_with_x(b - 1, 1, t2_mx, i - 1, on_vector=b == GRAPHS and i == PACK)
             if b < GRAPHS:
                 right_grouped = work.tile([P, NODES, PACK], BF16, align_bytes=64)
-                nc.vector.tensor_copy(
-                    out=right_grouped[:].rearrange("p (u w) t -> p u w t", u=PACK),
-                    in_=a_hat[b][:].rearrange("p t (w u) -> p u w t", u=PACK),
-                )
+                for h in range(2):
+                    cols = slice(h * 2 * P, (h + 1) * 2 * P)
+                    nc.vector.tensor_copy(
+                        out=right_grouped[:, cols, :].rearrange("p (e w) t -> p e w t", e=2),
+                        in_=a_hat[b][:, :, cols].rearrange("p t (w e) -> p e w t", e=2),
+                    )
                 left[b] = mx_tiles("left")
                 quantise(left[b], left_grouped[b], everything)
                 right = mx_tiles("right")

@@ -60,10 +60,8 @@ def tile_dygcn_pa_kernel(tc, A, x, out):
         nc.vector.memset(eye_grouped[:].rearrange("p i w t -> p (i w t)").bitcast(F32), 0.0)
         for e in range(2):
             nc.vector.tensor_copy(out=eye_pairs[:, e, e : 2 * P : 2], in_=ident_f32[:])
-        ident_bf16 = consts.tile([P, P], BF16)
 
         def finish_constants():
-            nc.vector.tensor_copy(out=ident_bf16[:], in_=ident_f32[:])
             for i in range(PACK):
                 nc.vector.tensor_copy(out=eye_grouped[:, i, :, i], in_=ident_f32[:])
 
@@ -163,28 +161,14 @@ def tile_dygcn_pa_kernel(tc, A, x, out):
                 nc.scalar.copy(out=res[:], in_=acc[:])
             nc.sync.dma_start(out=out[b, which].rearrange("(w i) f -> i w f", i=PACK)[c], in_=res[:])
 
-        def regroup_x(b):
+        def start_x(b):
             x_grouped[b] = work.tile([P, FEATS, PACK], BF16, name="x_grouped", align_bytes=64)
-            if b == 0:
-                nc.vector.tensor_copy(
-                    out=x_grouped[b][:].rearrange("p (c i) t -> p c t i", i=4),
-                    in_=x_raw[b][:].rearrange("p t (c i) -> p c t i", i=4),
-                )
-                return
-            for f0 in range(0, FEATS, 2 * P):
-                gathered = psum.tile([P, 2, P, PACK], BF16, tag="bank", name="gathered")
-                for k in range(2):
-                    nc.tensor.matmul(
-                        out=gathered[:, k, :, :],
-                        lhsT=ident_bf16[:],
-                        rhs=x_raw[b][:, :, f0 + k * P : f0 + (k + 1) * P].rearrange("p t f -> p f t"),
-                        start=True,
-                        stop=True,
-                    )
-                nc.scalar.copy(
-                    out=x_grouped[b][:, f0 : f0 + 2 * P, :].rearrange("p f t -> p (f t)").bitcast(F32),
-                    in_=gathered[:].rearrange("p k f t -> p (k f t)").bitcast(F32),
-                )
+
+        def regroup_x(b, copy, cols):
+            copy(
+                out=x_grouped[b][:, cols, :].rearrange("p (c i) t -> p c t i", i=4),
+                in_=x_raw[b][:, :, cols].rearrange("p t (c i) -> p c t i", i=4),
+            )
 
         def quantise_x(b):
             x_mx[b] = mx_tiles("x")
@@ -204,7 +188,8 @@ def tile_dygcn_pa_kernel(tc, A, x, out):
         factors(0)
         factors_row(0)
         finish_constants()
-        regroup_x(0)
+        start_x(0)
+        regroup_x(0, nc.vector.tensor_copy, everything)
         for b in range(GRAPHS + 1):
             ahead = b + 1 < GRAPHS
             if ahead:
@@ -222,8 +207,10 @@ def tile_dygcn_pa_kernel(tc, A, x, out):
                 quantise_x(0)
             if ahead:
                 factors(b + 1)
-                regroup_x(b + 1)
-                factors_row(b + 1)
+                start_x(b + 1)
+                regroup_x(b + 1, nc.scalar.copy, slice(FEATS // 2, FEATS))
+                if b == 0:
+                    factors_row(1)
             if b >= 1:
                 t2_grouped = work.tile([P, NODES, PACK], BF16, align_bytes=64)
                 t2_mx = mx_tiles("t2")
@@ -240,6 +227,8 @@ def tile_dygcn_pa_kernel(tc, A, x, out):
                     if i >= 1:
                         quantise(t2_mx, t2_grouped, block(i - 1))
                         product_with_x(b - 1, 1, t2_mx, i - 1, on_vector=b == GRAPHS and i == PACK)
+                if ahead:
+                    factors_row(b + 1)
             if b < GRAPHS:
                 right_grouped = work.tile([P, NODES, PACK], BF16, align_bytes=64)
                 for h in range(2):
@@ -250,6 +239,8 @@ def tile_dygcn_pa_kernel(tc, A, x, out):
                     )
                 left[b] = mx_tiles("left")
                 quantise(left[b], left_grouped[b], everything)
+                if ahead:
+                    regroup_x(b + 1, nc.vector.tensor_copy, slice(0, FEATS // 2))
                 right = mx_tiles("right")
                 quantise(right, right_grouped, everything)
                 for c in range(PACK):

@@ -95,6 +95,7 @@ def tile_dygcn_pa_kernel(tc, A, x, out):
         r_row = {}
         a_hat = {}
         left_grouped = {}
+        right_grouped = {}
         flipped = {}
         left = {}
         x_mx = {}
@@ -128,6 +129,7 @@ def tile_dygcn_pa_kernel(tc, A, x, out):
                 nc.tensor.transpose(r_row[b][:, t // 2, :, t % 2], r[b][:, t : t + 1].to_broadcast([P, P]), ident_f32[:])
 
         def start_normalise(b):
+            right_grouped[b] = work.tile([P, NODES, PACK], BF16, name="right_grouped", align_bytes=64)
             a_hat[b] = work.tile([P, PACK, NODES], BF16, name="a_hat")
             left_grouped[b] = work.tile([P, NODES, PACK], BF16, name="left_grouped", align_bytes=64)
 
@@ -161,6 +163,9 @@ def tile_dygcn_pa_kernel(tc, A, x, out):
                 nc.scalar.copy(out=res[:], in_=acc[:])
             nc.sync.dma_start(out=out[b, which].rearrange("(w i) f -> i w f", i=PACK)[c], in_=res[:])
 
+        def scalar_share(b):
+            return slice(0 if b == GRAPHS - 1 else FEATS // 2, FEATS)
+
         def start_x(b):
             x_grouped[b] = work.tile([P, FEATS, PACK], BF16, name="x_grouped", align_bytes=64)
 
@@ -168,6 +173,13 @@ def tile_dygcn_pa_kernel(tc, A, x, out):
             copy(
                 out=x_grouped[b][:, cols, :].rearrange("p (c i) t -> p c t i", i=4),
                 in_=x_raw[b][:, :, cols].rearrange("p t (c i) -> p c t i", i=4),
+            )
+
+        def regroup_right(b, copy, h):
+            cols = slice(h * 2 * P, (h + 1) * 2 * P)
+            copy(
+                out=right_grouped[b][:, cols, :].rearrange("p (e w) t -> p e w t", e=2),
+                in_=a_hat[b][:, :, cols].rearrange("p t (w e) -> p e w t", e=2),
             )
 
         def quantise_x(b):
@@ -203,12 +215,14 @@ def tile_dygcn_pa_kernel(tc, A, x, out):
                     if ahead and b > 0:
                         positive_part(b + 1, t)
                     normalise(b, t)
+            if b == GRAPHS - 1:
+                regroup_right(b, nc.scalar.copy, 1)
             if b == 0:
                 quantise_x(0)
             if ahead:
                 factors(b + 1)
                 start_x(b + 1)
-                regroup_x(b + 1, nc.scalar.copy, slice(FEATS // 2, FEATS))
+                regroup_x(b + 1, nc.scalar.copy, scalar_share(b + 1))
                 if b == 0:
                     factors_row(1)
             if b >= 1:
@@ -230,19 +244,15 @@ def tile_dygcn_pa_kernel(tc, A, x, out):
                 if ahead:
                     factors_row(b + 1)
             if b < GRAPHS:
-                right_grouped = work.tile([P, NODES, PACK], BF16, align_bytes=64)
-                for h in range(2):
-                    cols = slice(h * 2 * P, (h + 1) * 2 * P)
-                    nc.vector.tensor_copy(
-                        out=right_grouped[:, cols, :].rearrange("p (e w) t -> p e w t", e=2),
-                        in_=a_hat[b][:, :, cols].rearrange("p t (w e) -> p e w t", e=2),
-                    )
+                regroup_right(b, nc.vector.tensor_copy, 0)
+                if ahead:
+                    regroup_right(b, nc.vector.tensor_copy, 1)
                 left[b] = mx_tiles("left")
                 quantise(left[b], left_grouped[b], everything)
-                if ahead:
-                    regroup_x(b + 1, nc.vector.tensor_copy, slice(0, FEATS // 2))
+                if ahead and scalar_share(b + 1).start > 0:
+                    regroup_x(b + 1, nc.vector.tensor_copy, slice(0, scalar_share(b + 1).start))
                 right = mx_tiles("right")
-                quantise(right, right_grouped, everything)
+                quantise(right, right_grouped[b], everything)
                 for c in range(PACK):
                     if c == 2 and not ahead:
                         square(b, right)

@@ -54,16 +54,9 @@ def tile_dygcn_pa_kernel(tc, A, x, out):
         nc.scalar.activation(out=warm[:], in_=warm[:], func=ACT.Abs_reciprocal_sqrt)
         ident_f32 = consts.tile([P, P], F32)
         make_identity(nc, ident_f32[:])
-        eye_pairs = consts.tile([P, 2, 2 * P], F32)
-        nc.vector.memset(eye_pairs[:], 0.0)
-        eye_grouped = consts.tile([P, PACK, P, PACK], BF16)
-        nc.vector.memset(eye_grouped[:].rearrange("p i w t -> p (i w t)").bitcast(F32), 0.0)
-        for e in range(2):
-            nc.vector.tensor_copy(out=eye_pairs[:, e, e : 2 * P : 2], in_=ident_f32[:])
-
-        def finish_constants():
-            for i in range(PACK):
-                nc.vector.tensor_copy(out=eye_grouped[:, i, :, i], in_=ident_f32[:])
+        eye_wide = consts.tile([P, NODES + PACK], F32)
+        nc.vector.memset(eye_wide[:], 0.0)
+        nc.vector.tensor_copy(out=eye_wide[:, PACK : NODES + PACK : PACK], in_=ident_f32[:])
 
         def mx_tiles(name):
             codes = operands.tile([P, NODES], U32, name=name + "_codes", align_bytes=64)
@@ -116,16 +109,22 @@ def tile_dygcn_pa_kernel(tc, A, x, out):
                 )
             else:
                 nc.scalar.activation(out=relu_out, in_=relu_in, func=ACT.Relu, accum_out=total)
-            half = pos[b][:, t, (t // 2) * 2 * P : (t // 2 + 1) * 2 * P]
-            nc.gpsimd.tensor_tensor(out=half, in0=half, in1=eye_pairs[:, t % 2, :], op=ALU.add)
+            first = (t // 2) * 2 * P + t % 2
+            diagonal = pos[b][:, t, first : (t // 2 + 1) * 2 * P : 2]
+            nc.gpsimd.tensor_tensor(out=diagonal, in0=diagonal, in1=ident_f32[:], op=ALU.add)
 
-        def factors(b):
+        def start_factors(b):
             r[b] = work.tile([P, PACK], F32, name="r")
-            nc.scalar.activation(out=r[b][:], in_=row_sum[b][:], func=ACT.Abs_reciprocal_sqrt, bias=1.0)
 
-        def factors_row(b):
-            r_row[b] = psum.tile([P, 2, P, 2], F32, tag="bank", name="r_row")
-            for t in range(PACK):
+        def factors(b, rows):
+            nc.scalar.activation(
+                out=r[b][:, rows], in_=row_sum[b][:, rows], func=ACT.Abs_reciprocal_sqrt, bias=1.0
+            )
+
+        def factors_row(b, rows):
+            if rows.start == 0:
+                r_row[b] = psum.tile([P, 2, P, 2], F32, tag="bank", name="r_row")
+            for t in range(rows.start, rows.stop):
                 nc.tensor.transpose(r_row[b][:, t // 2, :, t % 2], r[b][:, t : t + 1].to_broadcast([P, P]), ident_f32[:])
 
         def start_normalise(b):
@@ -153,15 +152,15 @@ def tile_dygcn_pa_kernel(tc, A, x, out):
                     in_=flipped[b][:].rearrange("p s h w -> p s w h"),
                 )
 
-        def product_with_x(b, which, operand, c, on_vector=False):
-            acc = psum.tile([P, FEATS], F32, tag="bank", name="product")
-            multiply(acc[:], operand, block(c), x_mx[b], everything)
-            res = results.tile([P, FEATS], F32)
-            if on_vector:
-                nc.vector.tensor_copy(out=res[:], in_=acc[:])
-            else:
-                nc.scalar.copy(out=res[:], in_=acc[:])
-            nc.sync.dma_start(out=out[b, which].rearrange("(w i) f -> i w f", i=PACK)[c], in_=res[:])
+        def product_with_x(b, operand, c, feats=everything):
+            acc = psum.tile([P, feats.stop - feats.start], F32, tag="bank", name="product")
+            multiply(acc[:], operand, block(c), x_mx[b], feats)
+            return acc
+
+        def store_product(b, which, c, acc, copy=nc.scalar.copy, feats=everything):
+            res = results.tile([P, feats.stop - feats.start], F32)
+            copy(out=res[:], in_=acc[:])
+            nc.sync.dma_start(out=out[b, which].rearrange("(w i) f -> i w f", i=PACK)[c, :, feats], in_=res[:])
 
         def scalar_share(b):
             return slice(0 if b == GRAPHS - 1 else FEATS // 2, FEATS)
@@ -195,13 +194,15 @@ def tile_dygcn_pa_kernel(tc, A, x, out):
                 squares[b].append(acc)
 
         start_positive_part(0)
-        for t in range(PACK):
-            positive_part(0, t, on_vector=t % 2 == 1)
-        factors(0)
-        factors_row(0)
-        finish_constants()
+        start_factors(0)
         start_x(0)
-        regroup_x(0, nc.vector.tensor_copy, everything)
+        for rows in (slice(0, 2), slice(2, 4)):
+            for t in range(rows.start, rows.stop):
+                positive_part(0, t, on_vector=t == rows.start)
+            factors(0, rows)
+            factors_row(0, rows)
+        regroup_x(0, nc.vector.tensor_copy, slice(0, FEATS // 2))
+        regroup_x(0, nc.scalar.copy, slice(FEATS // 2, FEATS))
         for b in range(GRAPHS + 1):
             ahead = b + 1 < GRAPHS
             if ahead:
@@ -220,11 +221,12 @@ def tile_dygcn_pa_kernel(tc, A, x, out):
             if b == 0:
                 quantise_x(0)
             if ahead:
-                factors(b + 1)
+                start_factors(b + 1)
+                factors(b + 1, slice(0, PACK))
                 start_x(b + 1)
                 regroup_x(b + 1, nc.scalar.copy, scalar_share(b + 1))
                 if b == 0:
-                    factors_row(1)
+                    factors_row(1, slice(0, PACK))
             if b >= 1:
                 t2_grouped = work.tile([P, NODES, PACK], BF16, align_bytes=64)
                 t2_mx = mx_tiles("t2")
@@ -234,15 +236,24 @@ def tile_dygcn_pa_kernel(tc, A, x, out):
                             out=t2_grouped[:, block(i), :],
                             in0=squares[b - 1][i][:].rearrange("p t w -> p w t"),
                             scalar=2.0,
-                            in1=eye_grouped[:, i, :, :],
+                            in1=eye_wide[:, PACK - i : NODES + PACK - i].rearrange("p (w t) -> p w t", t=PACK),
                             op0=ALU.mult,
                             op1=ALU.subtract,
                         )
                     if i >= 1:
                         quantise(t2_mx, t2_grouped, block(i - 1))
-                        product_with_x(b - 1, 1, t2_mx, i - 1, on_vector=b == GRAPHS and i == PACK)
+                        if b < GRAPHS or i < PACK - 1:
+                            store_product(b - 1, 1, i - 1, product_with_x(b - 1, t2_mx, i - 1))
+                        elif i == PACK - 1:
+                            last_but_one = product_with_x(b - 1, t2_mx, i - 1)
+                        else:
+                            halves = [slice(0, FEATS // 2), slice(FEATS // 2, FEATS)]
+                            last = [product_with_x(b - 1, t2_mx, i - 1, feats) for feats in halves]
+                            store_product(b - 1, 1, i - 2, last_but_one, nc.vector.tensor_copy)
+                            store_product(b - 1, 1, i - 1, last[0], nc.scalar.copy, halves[0])
+                            store_product(b - 1, 1, i - 1, last[1], nc.vector.tensor_copy, halves[1])
                 if ahead:
-                    factors_row(b + 1)
+                    factors_row(b + 1, slice(0, PACK))
             if b < GRAPHS:
                 regroup_right(b, nc.vector.tensor_copy, 0)
                 if ahead:
@@ -256,7 +267,7 @@ def tile_dygcn_pa_kernel(tc, A, x, out):
                 for c in range(PACK):
                     if c == 2 and not ahead:
                         square(b, right)
-                    product_with_x(b, 0, left[b], c)
+                    store_product(b, 0, c, product_with_x(b, left[b], c))
                 if ahead:
                     square(b, right)
                 if ahead:

@@ -28,7 +28,8 @@ def tile_dygcn_pa_kernel(tc, A, x, out):
         work = ctx.enter_context(tc.tile_pool(name="work", bufs=2))
         operands = ctx.enter_context(tc.tile_pool(name="operands", bufs=3))
         results = ctx.enter_context(tc.tile_pool(name="results", bufs=12))
-        psum = ctx.enter_context(tc.psum_pool(name="psum", bufs=8))
+        psum = ctx.enter_context(tc.psum_pool(name="psum", bufs=7))
+        psum_row = ctx.enter_context(tc.psum_pool(name="psum_row", bufs=1))
         ctx.enter_context(tc.manual_schedule())
 
         def block(i):
@@ -54,6 +55,8 @@ def tile_dygcn_pa_kernel(tc, A, x, out):
         nc.scalar.activation(out=warm[:], in_=warm[:], func=ACT.Abs_reciprocal_sqrt)
         ident_f32 = consts.tile([P, P], F32)
         make_identity(nc, ident_f32[:])
+        ident_bf16 = consts.tile([P, P], BF16)
+        nc.vector.tensor_copy(out=ident_bf16[:], in_=ident_f32[:])
         eye_wide = consts.tile([P, NODES + PACK], F32)
         nc.vector.memset(eye_wide[:], 0.0)
         nc.vector.tensor_copy(out=eye_wide[:, PACK : NODES + PACK : PACK], in_=ident_f32[:])
@@ -93,6 +96,7 @@ def tile_dygcn_pa_kernel(tc, A, x, out):
         left = {}
         x_mx = {}
         x_grouped = {}
+        x_gathered = {}
         squares = {}
 
         def start_positive_part(b):
@@ -123,7 +127,7 @@ def tile_dygcn_pa_kernel(tc, A, x, out):
 
         def factors_row(b, rows):
             if rows.start == 0:
-                r_row[b] = psum.tile([P, 2, P, 2], F32, tag="bank", name="r_row")
+                r_row[b] = psum_row.tile([P, 2, P, 2], F32, name="r_row")
             for t in range(rows.start, rows.stop):
                 nc.tensor.transpose(r_row[b][:, t // 2, :, t % 2], r[b][:, t : t + 1].to_broadcast([P, P]), ident_f32[:])
 
@@ -162,9 +166,6 @@ def tile_dygcn_pa_kernel(tc, A, x, out):
             copy(out=res[:], in_=acc[:])
             nc.sync.dma_start(out=out[b, which].rearrange("(w i) f -> i w f", i=PACK)[c, :, feats], in_=res[:])
 
-        def scalar_share(b):
-            return slice(0 if b == GRAPHS - 1 else FEATS // 2, FEATS)
-
         def start_x(b):
             x_grouped[b] = work.tile([P, FEATS, PACK], BF16, name="x_grouped", align_bytes=64)
 
@@ -173,6 +174,27 @@ def tile_dygcn_pa_kernel(tc, A, x, out):
                 out=x_grouped[b][:, cols, :].rearrange("p (c i) t -> p c t i", i=4),
                 in_=x_raw[b][:, :, cols].rearrange("p t (c i) -> p c t i", i=4),
             )
+
+        def gather_x(b):
+            x_gathered[b] = []
+            for k in range(2):
+                gathered = psum.tile([P, 2 * P, PACK], BF16, tag="bank", name="gathered")
+                for t in range(0, PACK, 2):
+                    nc.tensor.matmul(
+                        out=gathered[:, :, t : t + 2].rearrange("p f t -> p t f"),
+                        lhsT=ident_bf16[:],
+                        rhs=x_raw[b][:, t : t + 2, k * 2 * P : (k + 1) * 2 * P],
+                        start=True,
+                        stop=True,
+                    )
+                x_gathered[b].append(gathered)
+
+        def empty_gathered_x(b):
+            for k in range(2):
+                nc.scalar.copy(
+                    out=x_grouped[b][:, k * 2 * P : (k + 1) * 2 * P, :].rearrange("p f t -> p (f t)").bitcast(F32),
+                    in_=x_gathered[b][k][:].rearrange("p f t -> p (f t)").bitcast(F32),
+                )
 
         def regroup_right(b, copy, h):
             cols = slice(h * 2 * P, (h + 1) * 2 * P)
@@ -193,6 +215,11 @@ def tile_dygcn_pa_kernel(tc, A, x, out):
                     multiply(acc[:, t, :], right, block(t), left[b], block(i))
                 squares[b].append(acc)
 
+        def multiply_t2(b, t2_mx, t2_grouped, i):
+            quantise(t2_mx, t2_grouped, slice(i * P, (i + 2) * P))
+            for bank in (i, i + 1):
+                store_product(b, 1, bank, product_with_x(b, t2_mx, bank))
+
         start_positive_part(0)
         start_factors(0)
         start_x(0)
@@ -207,61 +234,65 @@ def tile_dygcn_pa_kernel(tc, A, x, out):
             ahead = b + 1 < GRAPHS
             if ahead:
                 start_positive_part(b + 1)
-            if b == 0:
                 for t in range(PACK):
-                    positive_part(1, t)
+                    positive_part(b + 1, t)
+                if b > 0:
+                    gather_x(b + 1)
             if b < GRAPHS:
                 start_normalise(b)
                 for t in range(PACK):
-                    if ahead and b > 0:
-                        positive_part(b + 1, t)
                     normalise(b, t)
             if b == GRAPHS - 1:
                 regroup_right(b, nc.scalar.copy, 1)
             if b == 0:
                 quantise_x(0)
             if ahead:
+                if b == 0:
+                    gather_x(1)
                 start_factors(b + 1)
                 factors(b + 1, slice(0, PACK))
                 start_x(b + 1)
-                regroup_x(b + 1, nc.scalar.copy, scalar_share(b + 1))
+                empty_gathered_x(b + 1)
                 if b == 0:
                     factors_row(1, slice(0, PACK))
             if b >= 1:
                 t2_grouped = work.tile([P, NODES, PACK], BF16, align_bytes=64)
                 t2_mx = mx_tiles("t2")
-                for i in range(PACK + 1):
-                    if i < PACK:
-                        nc.vector.scalar_tensor_tensor(
-                            out=t2_grouped[:, block(i), :],
-                            in0=squares[b - 1][i][:].rearrange("p t w -> p w t"),
-                            scalar=2.0,
-                            in1=eye_wide[:, PACK - i : NODES + PACK - i].rearrange("p (w t) -> p w t", t=PACK),
-                            op0=ALU.mult,
-                            op1=ALU.subtract,
-                        )
-                    if i >= 1:
+                for i in range(PACK):
+                    nc.vector.scalar_tensor_tensor(
+                        out=t2_grouped[:, block(i), :],
+                        in0=squares[b - 1][i][:].rearrange("p t w -> p w t"),
+                        scalar=2.0,
+                        in1=eye_wide[:, PACK - i : NODES + PACK - i].rearrange("p (w t) -> p w t", t=PACK),
+                        op0=ALU.mult,
+                        op1=ALU.subtract,
+                    )
+                    if b < GRAPHS:
+                        if i == 2:
+                            multiply_t2(b - 1, t2_mx, t2_grouped, 0)
+                    elif i >= 1:
                         quantise(t2_mx, t2_grouped, block(i - 1))
-                        if b < GRAPHS or i < PACK - 1:
+                        if i < PACK - 1:
                             store_product(b - 1, 1, i - 1, product_with_x(b - 1, t2_mx, i - 1))
-                        elif i == PACK - 1:
-                            last_but_one = product_with_x(b - 1, t2_mx, i - 1)
                         else:
-                            halves = [slice(0, FEATS // 2), slice(FEATS // 2, FEATS)]
-                            last = [product_with_x(b - 1, t2_mx, i - 1, feats) for feats in halves]
-                            store_product(b - 1, 1, i - 2, last_but_one, nc.vector.tensor_copy)
-                            store_product(b - 1, 1, i - 1, last[0], nc.scalar.copy, halves[0])
-                            store_product(b - 1, 1, i - 1, last[1], nc.vector.tensor_copy, halves[1])
-                if ahead:
-                    factors_row(b + 1, slice(0, PACK))
+                            last_but_one = product_with_x(b - 1, t2_mx, i - 1)
+            if b == GRAPHS:
+                quantise(t2_mx, t2_grouped, block(PACK - 1))
+                halves = [slice(0, FEATS // 2), slice(FEATS // 2, FEATS)]
+                last = [product_with_x(b - 1, t2_mx, PACK - 1, feats) for feats in halves]
+                store_product(b - 1, 1, PACK - 2, last_but_one, nc.vector.tensor_copy)
+                store_product(b - 1, 1, PACK - 1, last[0], nc.scalar.copy, halves[0])
+                store_product(b - 1, 1, PACK - 1, last[1], nc.vector.tensor_copy, halves[1])
             if b < GRAPHS:
                 regroup_right(b, nc.vector.tensor_copy, 0)
+                if b >= 1:
+                    multiply_t2(b - 1, t2_mx, t2_grouped, 2)
+                    if ahead:
+                        factors_row(b + 1, slice(0, PACK))
                 if ahead:
                     regroup_right(b, nc.vector.tensor_copy, 1)
                 left[b] = mx_tiles("left")
                 quantise(left[b], left_grouped[b], everything)
-                if ahead and scalar_share(b + 1).start > 0:
-                    regroup_x(b + 1, nc.vector.tensor_copy, slice(0, scalar_share(b + 1).start))
                 right = mx_tiles("right")
                 quantise(right, right_grouped[b], everything)
                 for c in range(PACK):

from contextlib import ExitStack

import concourse.mybir as mybir
from concourse.masks import make_identity

BF16 = mybir.dt.bfloat16
F32 = mybir.dt.float32
U32 = mybir.dt.uint32
U8 = mybir.dt.uint8
FP8X4 = mybir.dt.float8_e4m3fn_x4
ACT = mybir.ActivationFunctionType
ALU = mybir.AluOpType

P = 128
PACK = 4
GRAPHS = 4
NODES = P * PACK
FEATS = 512

FLOPS = 3 * GRAPHS * 2 * NODES * NODES * FEATS


def tile_dygcn_pa_kernel(tc, A, x, out):
    nc = tc.nc
    with ExitStack() as ctx:
        consts = ctx.enter_context(tc.tile_pool(name="consts", bufs=1))
        loads = ctx.enter_context(tc.tile_pool(name="loads", bufs=GRAPHS))
        work = ctx.enter_context(tc.tile_pool(name="work", bufs=2))
        operands = ctx.enter_context(tc.tile_pool(name="operands", bufs=3))
        results = ctx.enter_context(tc.tile_pool(name="results", bufs=12))
        psum = ctx.enter_context(tc.psum_pool(name="psum", bufs=7))
        psum_row = ctx.enter_context(tc.psum_pool(name="psum_row", bufs=1))
        ctx.enter_context(tc.manual_schedule())

        def block(i):
            return slice(i * P, (i + 1) * P)

        a_raw = []
        x_raw = []
        for b in range(GRAPHS):
            a_tile = loads.tile([P, PACK, NODES], BF16, name="a_raw")
            rows = A[b].rearrange("(p t) m -> p t m", t=PACK)
            if b == 0:
                for t in range(PACK):
                    nc.sync.dma_start(out=a_tile[:, t, :], in_=rows[:, t, :])
            else:
                nc.sync.dma_start(out=a_tile[:], in_=rows)
            a_raw.append(a_tile)
            x_tile = loads.tile([P, PACK, FEATS], BF16, name="x_raw")
            nc.sync.dma_start(out=x_tile[:], in_=x[b].rearrange("(p t) f -> p t f", t=PACK))
            x_raw.append(x_tile)

        warm = consts.tile([P, 1], F32)
        nc.vector.memset(warm[:], 1.0)
        nc.scalar.activation(out=warm[:], in_=warm[:], func=ACT.Abs_reciprocal_sqrt)
        ident_f32 = consts.tile([P, P], F32)
        make_identity(nc, ident_f32[:])
        ident_bf16 = consts.tile([P, P], BF16)
        nc.vector.tensor_copy(out=ident_bf16[:], in_=ident_f32[:])
        eye_wide = consts.tile([P, NODES + PACK], F32)
        nc.vector.memset(eye_wide[:], 0.0)
        nc.vector.tensor_copy(out=eye_wide[:, PACK : NODES + PACK : PACK], in_=ident_f32[:])

        def mx_tiles(name):
            codes = operands.tile([P, NODES], U32, name=name + "_codes", align_bytes=64)
            scales = operands.tile([P, NODES], U8, name=name + "_scales", align_bytes=64)
            return codes, scales

        def quantise(operand, grouped, cols):
            nc.vector.quantize_mx(
                out=operand[0][:, cols].bitcast(FP8X4),
                scales=operand[1][:, cols],
                in_=grouped[:, cols, :].rearrange("p w t -> p (w t)"),
            )

        def multiply(acc, stationary, s_cols, moving, m_cols):
            nc.tensor.matmul_mx(
                out=acc,
                lhsT=stationary[0][:, s_cols].bitcast(FP8X4),
                lhsT_scale=stationary[1][:, s_cols],
                rhs=moving[0][:, m_cols].bitcast(FP8X4),
                rhs_scale=moving[1][:, m_cols],
                start=True,
                stop=True,
            )

        everything = slice(0, NODES)
        pos = {}
        row_sum = {}
        r = {}
        r_row = {}
        a_hat = {}
        left_grouped = {}
        right_grouped = {}
        flipped = {}
        left = {}
        x_mx = {}
        x_grouped = {}
        x_gathered = {}
        squares = {}

        def start_positive_part(b):
            pos[b] = work.tile([P, PACK, NODES], F32, name="pos")
            row_sum[b] = work.tile([P, PACK], F32, name="row_sum")

        def positive_part(b, t, on_vector=False):
            relu_out = pos[b][:, t, :].rearrange("p (h w e) -> p h w e", h=2, e=2)
            relu_in = a_raw[b][:, t, :].rearrange("p (w h e) -> p h w e", h=2, e=2)
            total = row_sum[b][:, t : t + 1]
            if on_vector:
                nc.vector.tensor_scalar(
                    out=relu_out, in0=relu_in, scalar1=0.0, scalar2=None, op0=ALU.max, op1=ALU.add, accum_out=total
                )
            else:
                nc.scalar.activation(out=relu_out, in_=relu_in, func=ACT.Relu, accum_out=total)
            first = (t // 2) * 2 * P + t % 2
            diagonal = pos[b][:, t, first : (t // 2 + 1) * 2 * P : 2]
            nc.gpsimd.tensor_tensor(out=diagonal, in0=diagonal, in1=ident_f32[:], op=ALU.add)

        def start_factors(b):
            r[b] = work.tile([P, PACK], F32, name="r")

        def factors(b, rows):
            nc.scalar.activation(
                out=r[b][:, rows], in_=row_sum[b][:, rows], func=ACT.Abs_reciprocal_sqrt, bias=1.0
            )

        def factors_row(b, rows):
            if rows.start == 0:
                r_row[b] = psum_row.tile([P, 2, P, 2], F32, name="r_row")
            for t in range(rows.start, rows.stop):
                nc.tensor.transpose(r_row[b][:, t // 2, :, t % 2], r[b][:, t : t + 1].to_broadcast([P, P]), ident_f32[:])

        def start_normalise(b):
            right_grouped[b] = work.tile([P, NODES, PACK], BF16, name="right_grouped", align_bytes=64)
            a_hat[b] = work.tile([P, PACK, NODES], BF16, name="a_hat")
            left_grouped[b] = work.tile([P, NODES, PACK], BF16, name="left_grouped", align_bytes=64)

        def normalise(b, t):
            nc.vector.scalar_tensor_tensor(
                out=a_hat[b][:, t, :],
                in0=pos[b][:, t, :],
                scalar=r[b][:, t : t + 1],
                in1=r_row[b][:].rearrange("p h w e -> p (h w e)"),
                op0=ALU.mult,
                op1=ALU.mult,
            )
            words = a_hat[b][:, t, :].bitcast(F32)
            if t % 2 == 0:
                flipped[b] = psum.tile([P, 2, 2, P], F32, tag="bank", name="flipped")
            for h in range(2):
                nc.tensor.transpose(flipped[b][:, t % 2, h, :], words[:, block(h)], ident_f32[:])
            if t % 2 == 1:
                nc.scalar.copy(
                    out=left_grouped[b][:, (t - 1) * P : (t + 1) * P, :].rearrange("p w u -> p (w u)").bitcast(F32).rearrange("p (s w h) -> p s w h", s=2, h=2),
                    in_=flipped[b][:].rearrange("p s h w -> p s w h"),
                )

        def product_with_x(b, operand, c, feats=everything):
            acc = psum.tile([P, feats.stop - feats.start], F32, tag="bank", name="product")
            multiply(acc[:], operand, block(c), x_mx[b], feats)
            return acc

        def store_product(b, which, c, acc, copy=nc.scalar.copy, feats=everything):
            res = results.tile([P, feats.stop - feats.start], F32)
            copy(out=res[:], in_=acc[:])
            nc.sync.dma_start(out=out[b, which].rearrange("(w i) f -> i w f", i=PACK)[c, :, feats], in_=res[:])

        def start_x(b):
            x_grouped[b] = work.tile([P, FEATS, PACK], BF16, name="x_grouped", align_bytes=64)

        def regroup_x(b, copy, cols):
            copy(
                out=x_grouped[b][:, cols, :].rearrange("p (c i) t -> p c t i", i=4),
                in_=x_raw[b][:, :, cols].rearrange("p t (c i) -> p c t i", i=4),
            )

        def gather_x(b):
            x_gathered[b] = []
            for k in range(2):
                gathered = psum.tile([P, 2 * P, PACK], BF16, tag="bank", name="gathered")
                for t in range(0, PACK, 2):
                    nc.tensor.matmul(
                        out=gathered[:, :, t : t + 2].rearrange("p f t -> p t f"),
                        lhsT=ident_bf16[:],
                        rhs=x_raw[b][:, t : t + 2, k * 2 * P : (k + 1) * 2 * P],
                        start=True,
                        stop=True,
                    )
                x_gathered[b].append(gathered)

        def empty_gathered_x(b):
            for k in range(2):
                nc.scalar.copy(
                    out=x_grouped[b][:, k * 2 * P : (k + 1) * 2 * P, :].rearrange("p f t -> p (f t)").bitcast(F32),
                    in_=x_gathered[b][k][:].rearrange("p f t -> p (f t)").bitcast(F32),
                )

        def regroup_right(b, copy, h):
            cols = slice(h * 2 * P, (h + 1) * 2 * P)
            copy(
                out=right_grouped[b][:, cols, :].rearrange("p (e w) t -> p e w t", e=2),
                in_=a_hat[b][:, :, cols].rearrange("p t (w e) -> p e w t", e=2),
            )

        def quantise_x(b):
            x_mx[b] = mx_tiles("x")
            quantise(x_mx[b], x_grouped[b], everything)

        def square(b, right):
            squares[b] = []
            for i in range(PACK):
                acc = psum.tile([P, PACK, P], F32, tag="bank", name="square")
                for t in range(PACK):
                    multiply(acc[:, t, :], right, block(t), left[b], block(i))
                squares[b].append(acc)

        def multiply_t2(b, t2_mx, t2_grouped, i):
            quantise(t2_mx, t2_grouped, slice(i * P, (i + 2) * P))
            for bank in (i, i + 1):
                store_product(b, 1, bank, product_with_x(b, t2_mx, bank))

        start_positive_part(0)
        start_factors(0)
        start_x(0)
        for rows in (slice(0, 2), slice(2, 4)):
            for t in range(rows.start, rows.stop):
                positive_part(0, t, on_vector=t == rows.start)
            factors(0, rows)
            factors_row(0, rows)
        regroup_x(0, nc.vector.tensor_copy, slice(0, FEATS // 2))
        regroup_x(0, nc.scalar.copy, slice(FEATS // 2, FEATS))
        for b in range(GRAPHS + 1):
            ahead = b + 1 < GRAPHS
            if ahead:
                start_positive_part(b + 1)
                for t in range(PACK):
                    positive_part(b + 1, t)
                if b > 0:
                    gather_x(b + 1)
            if b < GRAPHS:
                start_normalise(b)
                for t in range(PACK):
                    normalise(b, t)
            if b == GRAPHS - 1:
                regroup_right(b, nc.scalar.copy, 1)
            if b == 0:
                quantise_x(0)
            if ahead:
                if b == 0:
                    gather_x(1)
                start_factors(b + 1)
                factors(b + 1, slice(0, PACK))
                start_x(b + 1)
                empty_gathered_x(b + 1)
                if b == 0:
                    factors_row(1, slice(0, PACK))
            if b >= 1:
                t2_grouped = work.tile([P, NODES, PACK], BF16, align_bytes=64)
                t2_mx = mx_tiles("t2")
                for i in range(PACK):
                    nc.vector.scalar_tensor_tensor(
                        out=t2_grouped[:, block(i), :],
                        in0=squares[b - 1][i][:].rearrange("p t w -> p w t"),
                        scalar=2.0,
                        in1=eye_wide[:, PACK - i : NODES + PACK - i].rearrange("p (w t) -> p w t", t=PACK),
                        op0=ALU.mult,
                        op1=ALU.subtract,
                    )
                    if b < GRAPHS:
                        if i == 2:
                            multiply_t2(b - 1, t2_mx, t2_grouped, 0)
                    elif i >= 1:
                        quantise(t2_mx, t2_grouped, block(i - 1))
                        if i < PACK - 1:
                            store_product(b - 1, 1, i - 1, product_with_x(b - 1, t2_mx, i - 1))
                        else:
                            last_but_one = product_with_x(b - 1, t2_mx, i - 1)
            if b == GRAPHS:
                quantise(t2_mx, t2_grouped, block(PACK - 1))
                halves = [slice(0, FEATS // 2), slice(FEATS // 2, FEATS)]
                last = [product_with_x(b - 1, t2_mx, PACK - 1, feats) for feats in halves]
                store_product(b - 1, 1, PACK - 2, last_but_one, nc.vector.tensor_copy)
                store_product(b - 1, 1, PACK - 1, last[0], nc.scalar.copy, halves[0])
                store_product(b - 1, 1, PACK - 1, last[1], nc.vector.tensor_copy, halves[1])
            if b < GRAPHS:
                regroup_right(b, nc.vector.tensor_copy, 0)
                if b >= 1:
                    multiply_t2(b - 1, t2_mx, t2_grouped, 2)
                    if ahead:
                        factors_row(b + 1, slice(0, PACK))
                if ahead:
                    regroup_right(b, nc.vector.tensor_copy, 1)
                left[b] = mx_tiles("left")
                quantise(left[b], left_grouped[b], everything)
                right = mx_tiles("right")
                quantise(right, right_grouped[b], everything)
                for c in range(PACK):
                    if c == 2 and not ahead:
                        square(b, right)
                    store_product(b, 0, c, product_with_x(b, left[b], c))
                if ahead:
                    square(b, right)
                if ahead:
                    quantise_x(b + 1)
